import numpy as np
import ml_dtypes


def mxq(x, axis, fmt="e4m3"):
    dtype, down = {"e4m3": (ml_dtypes.float8_e4m3fn, 7), "e5m2": (ml_dtypes.float8_e5m2, 14)}[fmt]
    v = np.moveaxis(np.asarray(x, np.float32).astype(ml_dtypes.bfloat16).astype(np.float64), axis, -1)
    blocks = v.reshape(v.shape[:-1] + (-1, 32))
    amax = np.abs(blocks).max(-1, keepdims=True)
    byte = np.maximum(np.where(amax > 0, np.frexp(amax)[1] - 1 + 127, 0) - down, 1)
    scale = np.exp2(byte - 127.0)
    codes = (blocks / scale).astype(np.float32).astype(dtype).astype(np.float64)
    return np.moveaxis((codes * scale).reshape(v.shape), -1, axis)


WIDE = False


def mx_kscale(k):
    if not WIDE:
        return np.ones(k)
    levels = np.array([10, -10, 5, -5, 0])
    a = np.random.permutation(np.resize(levels, k // 512 * 4)).reshape(k // 512, 4)
    idx = np.arange(k)
    return np.exp2(a[idx // 512, idx % 128 // 32])


BF16 = ml_dtypes.bfloat16


def bf(x):
    return np.asarray(x, np.float32).astype(BF16)


def f64(x):
    return np.asarray(x).astype(np.float64)


B, S, D, H, QL, KVL, NOPE, ROPE, VD = 2, 256, 2048, 16, 1536, 512, 128, 128, 128
HALF = ROPE // 2
ROPE_BASE = 10000.0
EPS = 1e-6


def rmsnorm(x, w):
    return x * (1.0 / np.sqrt(np.mean(x * x, axis=-1, keepdims=True) + EPS)) * w


def rope_tables():
    inv_freq = 1.0 / ROPE_BASE ** (np.arange(HALF) / HALF)
    ang = np.arange(S)[:, None] * inv_freq
    return np.cos(ang), np.sin(ang)


def rope(x, cos, sin):
    x1, x2 = x[..., :HALF], x[..., HALF:]
    return np.concatenate([x1 * cos - x2 * sin, x1 * sin + x2 * cos], axis=-1)


def setup_inputs():
    s, t = mx_kscale(D), mx_kscale(KVL)
    return {
        "hidden_states": bf(np.random.standard_normal((B, S, D)) * s),
        "w_kv_a": bf(np.random.standard_normal((D, KVL + ROPE)) / np.sqrt(D) / s[:, None]),
        "kv_a_ln_w": bf((1.0 + 0.1 * np.random.standard_normal(KVL)) * t),
        "w_kv_b": bf(np.random.standard_normal((KVL, H * (NOPE + VD))) / np.sqrt(KVL) / t[:, None]),
    }


def reference(hidden_states, w_kv_a, kv_a_ln_w, w_kv_b):
    fused = mxq(f64(hidden_states), 2, "e4m3") @ mxq(f64(w_kv_a), 0, "e4m3")
    kv_c, k_pe = fused[..., :KVL], fused[..., KVL:]
    kv_n = rmsnorm(kv_c, f64(kv_a_ln_w))
    kv = (mxq(kv_n, 2, "e4m3") @ mxq(f64(w_kv_b), 0, "e4m3")).reshape(B, S, H, NOPE + VD)
    k_nope, v = kv[..., :NOPE], kv[..., NOPE:]
    cos, sin = rope_tables()
    k_pe = rope(k_pe, cos[None], sin[None])
    k = np.concatenate([k_nope, np.broadcast_to(k_pe[:, :, None, :], (B, S, H, ROPE))], axis=-1)
    return k, v

@@ -1,0 +1,370 @@
+import math
+from contextlib import ExitStack
+
+import concourse.mybir as mybir
+from concourse.masks import make_identity
+
+F32 = mybir.dt.float32
+BF16 = mybir.dt.bfloat16
+I32 = mybir.dt.int32
+U32 = mybir.dt.uint32
+U8 = mybir.dt.uint8
+FP8X4 = mybir.dt.float8_e4m3fn_x4
+ALU = mybir.AluOpType
+ACT = mybir.ActivationFunctionType
+
+P = 128
+PACK = 4
+K_PASS = P * PACK
+BANK = 512
+
+TOKENS = 512
+TOKEN_TILES = TOKENS // P
+D_MODEL = 2048
+PASSES_A = D_MODEL // K_PASS
+LATENT = 512
+ROPE = 128
+HALF = ROPE // 2
+HALF_LOG2 = 6
+assert 2**HALF_LOG2 == HALF
+FUSED = LATENT + ROPE
+HEADS = 16
+NOPE = 128
+V_DIM = 128
+HEAD_COLS = NOPE + V_DIM
+KV_COLS = HEADS * HEAD_COLS
+ROPE_BASE = 10000.0
+EPS = 1e-6
+
+PIECE_HEADS = 4
+PIECE_COLS = PIECE_HEADS * HEAD_COLS
+PIECES = HEADS // PIECE_HEADS
+BANKS_PER_PIECE = PIECE_COLS // BANK
+BANK_HEADS = BANK // HEAD_COLS
+
+RUN = 4
+A_SPLIT = FUSED // 2
+
+ROUND_MAGIC = 1.5 * 2.0**23
+
+FLOPS = 2 * TOKENS * D_MODEL * FUSED + 2 * TOKENS * LATENT * KV_COLS
+
+
+def regroup(copy, grouped, raw):
+    copy(
+        out=grouped.rearrange("p (c i) t -> p c t i", i=RUN),
+        in_=raw.rearrange("p t (c i) -> p c t i", i=RUN),
+    )
+
+
+def tile_mla_pb_kernel(tc, hidden_states, w_kv_a, kv_a_ln_w, w_kv_b, out_0, out_1):
+    nc = tc.nc
+    hidden = hidden_states.flatten_outer_dims()
+    k_out = out_0.rearrange("b s h c -> (b s) h c")
+    v_out = out_1.rearrange("b s h c -> (b s) h c")
+
+    with ExitStack() as ctx:
+        ctx.enter_context(tc.manual_schedule())
+        consts = ctx.enter_context(tc.tile_pool(name="consts", bufs=1))
+        resident = ctx.enter_context(tc.tile_pool(name="resident", bufs=1))
+        stage = ctx.enter_context(tc.tile_pool(name="stage", bufs=2))
+        pieces = ctx.enter_context(tc.tile_pool(name="pieces", bufs=6))
+        psum = ctx.enter_context(tc.psum_pool(name="psum", bufs=1))
+
+        gain_row = consts.tile([P, LATENT], BF16)
+        nc.vector.memset(gain_row[:], 0.0)
+        raw_a = []
+        for g in range(PASSES_A):
+            raw = resident.tile([P, PACK, FUSED], BF16, name="raw_a%d" % g)
+            rows = w_kv_a[g * K_PASS : (g + 1) * K_PASS, :]
+            nc.sync.dma_start(
+                out=raw[:].rearrange("p (u e) c -> p u e c", u=2),
+                in_=rows.rearrange("(u q e) c -> q u e c", u=2, e=2),
+            )
+            raw_a.append(raw)
+            if g == 0:
+                nc.sync.dma_start(out=gain_row[0:1, :], in_=kv_a_ln_w.unsqueeze(0))
+        x_rows = []
+        raw_b = []
+
+        def load_hidden(tt):
+            rows = resident.tile([P, D_MODEL], BF16, name="x_rows%d" % tt)
+            nc.sync.dma_start(out=rows[:], in_=hidden[tt * P : (tt + 1) * P, :])
+            x_rows.append(rows)
+
+        def load_b(j):
+            raw = resident.tile([P, PACK, PIECE_COLS], BF16, name="raw_b%d" % j)
+            cols = w_kv_b[:, j * PIECE_COLS : (j + 1) * PIECE_COLS]
+            nc.sync.dma_start(out=raw[:], in_=cols.rearrange("(t p) n -> p t n", p=P))
+            raw_b.append(raw)
+
+        load_hidden(0)
+        load_hidden(1)
+        load_b(0)
+        load_hidden(2)
+        load_hidden(3)
+        for j in range(1, PIECES):
+            load_b(j)
+
+        position = consts.tile([P, 2], I32)
+        nc.gpsimd.iota(position[:], pattern=[[P, 2]], base=0, channel_multiplier=1)
+        inv_freq = consts.tile([P, HALF], F32)
+        nc.vector.memset(inv_freq[:, 0:1], 1.0)
+        for level in range(HALF_LOG2):
+            width = 2**level
+            nc.vector.tensor_scalar(
+                out=inv_freq[:, width : 2 * width], in0=inv_freq[:, 0:width],
+                scalar1=ROPE_BASE ** (-width / HALF), scalar2=None, op0=ALU.mult,
+            )
+        position_turns = consts.tile([P, 2], F32)
+        nc.vector.tensor_scalar(
+            out=position_turns[:], in0=position[:], scalar1=1.0 / (2.0 * math.pi), scalar2=None,
+            op0=ALU.mult,
+        )
+        phases = (0.5, 0.25, 0.0)
+        turns = consts.tile([P, 2, len(phases), HALF], F32)
+        for a in range(2):
+            for i, phase in enumerate(phases):
+                nc.vector.tensor_scalar(
+                    out=turns[:, a, i, :], in0=inv_freq[:], scalar1=position_turns[:, a : a + 1],
+                    scalar2=phase, op0=ALU.mult, op1=ALU.add,
+                )
+        whole_turns = consts.tile([P, 2, len(phases), HALF], F32)
+        nc.vector.tensor_scalar(
+            out=whole_turns[:], in0=turns[:], scalar1=ROUND_MAGIC, scalar2=ROUND_MAGIC,
+            op0=ALU.add, op1=ALU.subtract,
+        )
+        part_turns = consts.tile([P, 2, len(phases), HALF], F32)
+        nc.vector.tensor_tensor(out=part_turns[:], in0=turns[:], in1=whole_turns[:], op=ALU.subtract)
+        table = consts.tile([P, 2, len(phases), HALF], F32)
+        nc.scalar.activation(out=table[:], in_=part_turns[:], func=ACT.Sin, scale=2.0 * math.pi)
+
+        square_sum = consts.tile([P, TOKEN_TILES], F32)
+        rms = consts.tile([P, TOKEN_TILES], F32)
+        inv_rms = consts.tile([P, TOKEN_TILES], F32)
+        nc.scalar.activation(out=rms[:, 0:1], in_=inv_freq[:, 0:1], func=ACT.Sqrt)
+
+        ident_f32 = consts.tile([P, P], F32)
+        make_identity(nc, ident_f32[:])
+        ident_bf16 = consts.tile([P, P], BF16)
+        make_identity(nc, ident_bf16[:])
+        ones = consts.tile([P, P], BF16)
+        nc.vector.memset(ones[:], 1.0)
+        gain_ps = psum.tile([P, LATENT], F32, tag="bank", bufs=4)
+        nc.tensor.matmul(out=gain_ps[:], lhsT=ones[:], rhs=gain_row[:], start=True, stop=True)
+        gain = consts.tile([P, LATENT], BF16)
+
+        a_codes = resident.tile([P, PASSES_A, FUSED], U32, align_bytes=64)
+        a_scales = resident.tile([P, PASSES_A, FUSED], U8, align_bytes=64)
+        grouped_a = []
+        for g in range(PASSES_A + 1):
+            if g < PASSES_A:
+                grouped = stage.tile([P, FUSED, PACK], BF16, align_bytes=64, tag="grouped_a")
+                regroup(nc.vector.tensor_copy, grouped[:, :A_SPLIT, :], raw_a[g][:, :, :A_SPLIT])
+                regroup(nc.scalar.copy, grouped[:, A_SPLIT:, :], raw_a[g][:, :, A_SPLIT:])
+                grouped_a.append(grouped)
+            if g == 0:
+                nc.vector.tensor_copy(out=gain[:], in_=gain_ps[:])
+            else:
+                for cols in (slice(0, LATENT), slice(LATENT, FUSED)):
+                    nc.vector.quantize_mx(
+                        out=a_codes[:, g - 1, cols].bitcast(FP8X4),
+                        scales=a_scales[:, g - 1, cols],
+                        in_=grouped_a[g - 1][:, cols, :].rearrange("p c t -> p (c t)"),
+                    )
+
+        x_codes = resident.tile([P, TOKEN_TILES, PASSES_A * P], U32, align_bytes=64)
+        x_scales = resident.tile([P, TOKEN_TILES, PASSES_A * P], U8, align_bytes=64)
+        n_codes = resident.tile([P, TOKEN_TILES, P], U32, align_bytes=64)
+        n_scales = resident.tile([P, TOKEN_TILES, P], U8, align_bytes=64)
+        b_codes = resident.tile([P, KV_COLS], U32, align_bytes=64)
+        b_scales = resident.tile([P, KV_COLS], U8, align_bytes=64)
+        grouped_x = {}
+        latent_ps = {}
+        rope_ps = {}
+        kv_n = {}
+        flipped_n = {}
+        grouped_n = {}
+        grouped_b = {}
+        k_pe = {}
+
+        def flip_hidden(tt):
+            words = x_rows[tt][:].bitcast(F32)
+            grouped_x[tt] = stage.tile(
+                [P, PASSES_A * P * PACK], BF16, align_bytes=64, name="grouped_x", tag="grouped_x"
+            )
+            grouped_words = grouped_x[tt][:].bitcast(F32).rearrange(
+                "p (g k u) -> p g k u", g=PASSES_A, u=2
+            )
+            for b in range(2):
+                flipped = psum.tile([P, 2, 2, P], F32, tag="bank", bufs=4)
+                for gg in range(2):
+                    for u in range(2):
+                        first = (2 * b + gg) * (K_PASS // 2) + u * P
+                        nc.tensor.transpose(
+                            flipped[:, gg, u, :], words[:, first : first + P], ident_f32[:]
+                        )
+                nc.scalar.copy(
+                    out=grouped_words[:, 2 * b : 2 * b + 2, :, :],
+                    in_=flipped[:].rearrange("p g u k -> p g k u"),
+                )
+
+        def quantise_hidden(tt):
+            nc.vector.quantize_mx(
+                out=x_codes[:, tt, :].bitcast(FP8X4), scales=x_scales[:, tt, :], in_=grouped_x[tt][:]
+            )
+
+        def first_product(tt):
+            latent_ps[tt] = psum.tile([P, LATENT], F32, name="latent_ps", tag="latent", bufs=2)
+            rope_ps[tt] = psum.tile([P, ROPE], F32, name="rope_ps", tag="rope", bufs=1)
+            for g in range(PASSES_A):
+                of_pass = slice(g * P, (g + 1) * P)
+                for acc, cols in (
+                    (latent_ps[tt], slice(0, LATENT)),
+                    (rope_ps[tt], slice(LATENT, FUSED)),
+                ):
+                    nc.tensor.matmul_mx(
+                        out=acc[:],
+                        lhsT=x_codes[:, tt, of_pass].bitcast(FP8X4),
+                        lhsT_scale=x_scales[:, tt, of_pass],
+                        rhs=a_codes[:, g, cols].bitcast(FP8X4),
+                        rhs_scale=a_scales[:, g, cols],
+                        start=(g == 0),
+                        stop=(g == PASSES_A - 1),
+                    )
+
+        def root_mean_square(tt):
+            squares = stage.tile([P, LATENT], BF16)
+            nc.scalar.activation(
+                out=squares[:], in_=latent_ps[tt][:], func=ACT.Square,
+                accum_out=square_sum[:, tt : tt + 1],
+            )
+            nc.scalar.activation(
+                out=rms[:, tt : tt + 1], in_=square_sum[:, tt : tt + 1], func=ACT.Sqrt,
+                bias=EPS, scale=1.0 / LATENT,
+            )
+
+        def normalise(tt):
+            nc.vector.reciprocal(out=inv_rms[:, tt : tt + 1], in_=rms[:, tt : tt + 1])
+            kv_n[tt] = stage.tile([P, LATENT], BF16, name="kv_n", tag="kv_n")
+            nc.vector.scalar_tensor_tensor(
+                out=kv_n[tt][:], in0=latent_ps[tt][:], scalar=inv_rms[:, tt : tt + 1], in1=gain[:],
+                op0=ALU.mult, op1=ALU.mult,
+            )
+
+        def flip_kv_n(tt):
+            flipped_n[tt] = psum.tile([P, PACK, P], BF16, name="flipped_n", tag="flipped_n", bufs=1)
+            for t in range(PACK):
+                nc.tensor.transpose(
+                    flipped_n[tt][:, t, :], kv_n[tt][:, t * P : (t + 1) * P], ident_bf16[:]
+                )
+
+        def regroup_kv_n(tt):
+            grouped_n[tt] = stage.tile([P, P, PACK], BF16, align_bytes=64, name="grouped_n", tag="grouped_n")
+            nc.scalar.copy(out=grouped_n[tt][:], in_=flipped_n[tt][:].rearrange("p t k -> p k t"))
+
+        def quantise_kv_n(tt):
+            nc.vector.quantize_mx(
+                out=n_codes[:, tt, :].bitcast(FP8X4),
+                scales=n_scales[:, tt, :],
+                in_=grouped_n[tt][:].rearrange("p k t -> p (k t)"),
+            )
+
+        def rotate(tt):
+            x = stage.tile([P, ROPE], F32, name="rope_x", tag="rope_x")
+            nc.scalar.copy(out=x[:], in_=rope_ps[tt][:])
+            a = tt % 2
+            x1 = x[:, 0:HALF].unsqueeze(1).to_broadcast([P, 2, HALF])
+            x2 = x[:, HALF:ROPE].unsqueeze(1).to_broadcast([P, 2, HALF])
+            from_x1 = stage.tile([P, 2, HALF], F32)
+            nc.gpsimd.tensor_tensor(out=from_x1[:], in0=x1, in1=table[:, a, 1:3, :], op=ALU.mult)
+            from_x2 = stage.tile([P, 2, HALF], F32)
+            nc.gpsimd.tensor_tensor(out=from_x2[:], in0=x2, in1=table[:, a, 0:2, :], op=ALU.mult)
+            k_pe[tt] = consts.tile([P, 2, HALF], F32, name="k_pe%d" % tt)
+            nc.gpsimd.tensor_tensor(out=k_pe[tt][:], in0=from_x1[:], in1=from_x2[:], op=ALU.add)
+
+        def bank_cols(j, b):
+            return slice(j * PIECE_COLS + b * BANK, j * PIECE_COLS + (b + 1) * BANK)
+
+        def regroup_b(j, b):
+            grouped_b[j, b] = stage.tile([P, BANK, PACK], BF16, align_bytes=64, name="grouped_b", tag="grouped_b")
+            regroup(nc.vector.tensor_copy, grouped_b[j, b][:], raw_b[j][:, :, b * BANK : (b + 1) * BANK])
+
+        def quantise_b(j, b):
+            nc.vector.quantize_mx(
+                out=b_codes[:, bank_cols(j, b)].bitcast(FP8X4),
+                scales=b_scales[:, bank_cols(j, b)],
+                in_=grouped_b[j, b][:].rearrange("p c t -> p (c t)"),
+            )
+
+        def prepare_b(j, turn):
+            if turn % 2 == 0:
+                regroup_b(j, turn // 2)
+            else:
+                quantise_b(j, turn // 2)
+
+        def second_product(j, tt):
+            if j + 1 < PIECES:
+                prepare_b(j + 1, tt)
+            k_piece = pieces.tile([P, PIECE_HEADS, NOPE + ROPE], F32)
+            v_piece = pieces.tile([P, PIECE_HEADS, V_DIM], F32)
+            nc.gpsimd.tensor_scalar(
+                out=k_piece[:, :, NOPE:],
+                in0=k_pe[tt][:].rearrange("p h c -> p (h c)").unsqueeze(1).to_broadcast(
+                    [P, PIECE_HEADS, ROPE]
+                ),
+                scalar1=1.0, scalar2=0.0, op0=ALU.mult, op1=ALU.add,
+            )
+            for b in range(BANKS_PER_PIECE):
+                kv_ps = psum.tile([P, BANK], F32, tag="bank", bufs=4)
+                nc.tensor.matmul_mx(
+                    out=kv_ps[:],
+                    lhsT=n_codes[:, tt, :].bitcast(FP8X4),
+                    lhsT_scale=n_scales[:, tt, :],
+                    rhs=b_codes[:, bank_cols(j, b)].bitcast(FP8X4),
+                    rhs_scale=b_scales[:, bank_cols(j, b)],
+                    start=True,
+                    stop=True,
+                )
+                kv = kv_ps[:].rearrange("p (h s c) -> p h s c", h=BANK_HEADS, s=2)
+                in_piece = slice(b * BANK_HEADS, (b + 1) * BANK_HEADS)
+                to_vector = tt % 2 == 1 and b == BANKS_PER_PIECE - 1
+                copy = nc.vector.tensor_copy if to_vector else nc.scalar.copy
+                copy(out=k_piece[:, in_piece, :NOPE], in_=kv[:, :, 0, :])
+                copy(out=v_piece[:, in_piece, :], in_=kv[:, :, 1, :])
+            tokens = slice(tt * P, (tt + 1) * P)
+            heads = slice(j * PIECE_HEADS, (j + 1) * PIECE_HEADS)
+            nc.sync.dma_start(out=k_out[tokens, heads, :], in_=k_piece[:])
+            nc.sync.dma_start(out=v_out[tokens, heads, :], in_=v_piece[:])
+
+        def is_tile(tt):
+            return 0 <= tt < TOKEN_TILES
+
+        flip_hidden(0)
+        flip_hidden(1)
+        quantise_hidden(0)
+        for step in range(TOKEN_TILES + 4):
+            if is_tile(step - 3):
+                quantise_kv_n(step - 3)
+            if is_tile(step - 1):
+                normalise(step - 1)
+            if is_tile(step + 1):
+                quantise_hidden(step + 1)
+            if step < TOKEN_TILES:
+                prepare_b(0, step)
+            if is_tile(step - 4):
+                second_product(0, step - 4)
+            if is_tile(step):
+                first_product(step)
+                root_mean_square(step)
+            if is_tile(step + 2):
+                flip_hidden(step + 2)
+            if is_tile(step - 2):
+                flip_kv_n(step - 2)
+                regroup_kv_n(step - 2)
+            if is_tile(step):
+                rotate(step)
+
+        for j in range(1, PIECES):
+            for tt in range(TOKEN_TILES):
+                second_product(j, tt)

@@ -31,30 +31,22 @@ FUSED = LATENT + ROPE
 HEADS = 16
 NOPE = 128
 V_DIM = 128
-HEAD_COLS = NOPE + V_DIM
-KV_COLS = HEADS * HEAD_COLS
+KINDS = 2
+KIND_K_NOPE = 0
+KIND_V = 1
 ROPE_BASE = 10000.0
 EPS = 1e-6
 
-PIECE_HEADS = 4
-PIECE_COLS = PIECE_HEADS * HEAD_COLS
+PIECE_HEADS = BANK // NOPE
+PIECE_COLS = PIECE_HEADS * (NOPE + V_DIM)
 PIECES = HEADS // PIECE_HEADS
-BANKS_PER_PIECE = PIECE_COLS // BANK
-BANK_HEADS = BANK // HEAD_COLS
 
 RUN = 4
 A_SPLIT = FUSED // 2
 
 ROUND_MAGIC = 1.5 * 2.0**23
 
-FLOPS = 2 * TOKENS * D_MODEL * FUSED + 2 * TOKENS * LATENT * KV_COLS
-
-
-def regroup(copy, grouped, raw):
-    copy(
-        out=grouped.rearrange("p (c i) t -> p c t i", i=RUN),
-        in_=raw.rearrange("p t (c i) -> p c t i", i=RUN),
-    )
+FLOPS = 2 * TOKENS * D_MODEL * FUSED + 2 * TOKENS * LATENT * HEADS * (NOPE + V_DIM)
 
 
 def tile_mla_pb_kernel(tc, hidden_states, w_kv_a, kv_a_ln_w, w_kv_b, out_0, out_1):
@@ -69,10 +61,17 @@ def tile_mla_pb_kernel(tc, hidden_states, w_kv_a, kv_a_ln_w, w_kv_b, out_0, out_
         resident = ctx.enter_context(tc.tile_pool(name="resident", bufs=1))
         stage = ctx.enter_context(tc.tile_pool(name="stage", bufs=2))
         pieces = ctx.enter_context(tc.tile_pool(name="pieces", bufs=6))
-        psum = ctx.enter_context(tc.psum_pool(name="psum", bufs=1))
+        psum = ctx.enter_context(tc.psum_pool(name="psum", bufs=4))
 
         gain_row = consts.tile([P, LATENT], BF16)
         nc.vector.memset(gain_row[:], 0.0)
+        x_rows = []
+        for tt in range(TOKEN_TILES):
+            rows = resident.tile([P, D_MODEL], BF16, name="x_rows%d" % tt)
+            nc.sync.dma_start(out=rows[:], in_=hidden[tt * P : (tt + 1) * P, :])
+            x_rows.append(rows)
+            if tt == 0:
+                nc.sync.dma_start(out=gain_row[0:1, :], in_=kv_a_ln_w.unsqueeze(0))
         raw_a = []
         for g in range(PASSES_A):
             raw = resident.tile([P, PACK, FUSED], BF16, name="raw_a%d" % g)
@@ -82,29 +81,12 @@ def tile_mla_pb_kernel(tc, hidden_states, w_kv_a, kv_a_ln_w, w_kv_b, out_0, out_
                 in_=rows.rearrange("(u q e) c -> q u e c", u=2, e=2),
             )
             raw_a.append(raw)
-            if g == 0:
-                nc.sync.dma_start(out=gain_row[0:1, :], in_=kv_a_ln_w.unsqueeze(0))
-        x_rows = []
         raw_b = []
-
-        def load_hidden(tt):
-            rows = resident.tile([P, D_MODEL], BF16, name="x_rows%d" % tt)
-            nc.sync.dma_start(out=rows[:], in_=hidden[tt * P : (tt + 1) * P, :])
-            x_rows.append(rows)
-
-        def load_b(j):
+        for j in range(PIECES):
             raw = resident.tile([P, PACK, PIECE_COLS], BF16, name="raw_b%d" % j)
             cols = w_kv_b[:, j * PIECE_COLS : (j + 1) * PIECE_COLS]
             nc.sync.dma_start(out=raw[:], in_=cols.rearrange("(t p) n -> p t n", p=P))
             raw_b.append(raw)
-
-        load_hidden(0)
-        load_hidden(1)
-        load_b(0)
-        load_hidden(2)
-        load_hidden(3)
-        for j in range(1, PIECES):
-            load_b(j)
 
         position = consts.tile([P, 2], I32)
         nc.gpsimd.iota(position[:], pattern=[[P, 2]], base=0, channel_multiplier=1)
@@ -150,75 +132,72 @@ def tile_mla_pb_kernel(tc, hidden_states, w_kv_a, kv_a_ln_w, w_kv_b, out_0, out_
         make_identity(nc, ident_bf16[:])
         ones = consts.tile([P, P], BF16)
         nc.vector.memset(ones[:], 1.0)
-        gain_ps = psum.tile([P, LATENT], F32, tag="bank", bufs=4)
+        gain_ps = psum.tile([P, LATENT], F32, tag="right")
         nc.tensor.matmul(out=gain_ps[:], lhsT=ones[:], rhs=gain_row[:], start=True, stop=True)
         gain = consts.tile([P, LATENT], BF16)
+        nc.vector.tensor_copy(out=gain[:], in_=gain_ps[:])
+
+        x_codes = resident.tile([P, TOKEN_TILES, PASSES_A * P], U32, align_bytes=64)
+        x_scales = resident.tile([P, TOKEN_TILES, PASSES_A * P], U8, align_bytes=64)
+        for tt in range(TOKEN_TILES):
+            words = x_rows[tt][:].bitcast(F32)
+            grouped_x = stage.tile([P, PASSES_A * P * PACK], BF16, align_bytes=64)
+            grouped_words = grouped_x[:].bitcast(F32).rearrange(
+                "p (g k u) -> p g k u", g=PASSES_A, u=2
+            )
+            for ring, copy, first_pass in (
+                ("left", nc.scalar.copy, 0),
+                ("right", nc.vector.tensor_copy, 2),
+            ):
+                flipped = psum.tile([P, 2, 2, P], F32, tag=ring)
+                for gg in range(2):
+                    for u in range(2):
+                        first = (first_pass + gg) * (K_PASS // 2) + u * P
+                        nc.tensor.transpose(
+                            flipped[:, gg, u, :], words[:, first : first + P], ident_f32[:]
+                        )
+                copy(
+                    out=grouped_words[:, first_pass : first_pass + 2, :, :],
+                    in_=flipped[:].rearrange("p g u k -> p g k u"),
+                )
+            nc.vector.quantize_mx(
+                out=x_codes[:, tt, :].bitcast(FP8X4), scales=x_scales[:, tt, :], in_=grouped_x[:]
+            )
 
         a_codes = resident.tile([P, PASSES_A, FUSED], U32, align_bytes=64)
         a_scales = resident.tile([P, PASSES_A, FUSED], U8, align_bytes=64)
         grouped_a = []
-        for g in range(PASSES_A + 1):
-            if g < PASSES_A:
-                grouped = stage.tile([P, FUSED, PACK], BF16, align_bytes=64, tag="grouped_a")
-                regroup(nc.vector.tensor_copy, grouped[:, :A_SPLIT, :], raw_a[g][:, :, :A_SPLIT])
-                regroup(nc.scalar.copy, grouped[:, A_SPLIT:, :], raw_a[g][:, :, A_SPLIT:])
-                grouped_a.append(grouped)
-            if g == 0:
-                nc.vector.tensor_copy(out=gain[:], in_=gain_ps[:])
-            else:
-                for cols in (slice(0, LATENT), slice(LATENT, FUSED)):
-                    nc.vector.quantize_mx(
-                        out=a_codes[:, g - 1, cols].bitcast(FP8X4),
-                        scales=a_scales[:, g - 1, cols],
-                        in_=grouped_a[g - 1][:, cols, :].rearrange("p c t -> p (c t)"),
-                    )
+        latent_ps = []
+        rope_ps = []
 
-        x_codes = resident.tile([P, TOKEN_TILES, PASSES_A * P], U32, align_bytes=64)
-        x_scales = resident.tile([P, TOKEN_TILES, PASSES_A * P], U8, align_bytes=64)
-        n_codes = resident.tile([P, TOKEN_TILES, P], U32, align_bytes=64)
-        n_scales = resident.tile([P, TOKEN_TILES, P], U8, align_bytes=64)
-        b_codes = resident.tile([P, KV_COLS], U32, align_bytes=64)
-        b_scales = resident.tile([P, KV_COLS], U8, align_bytes=64)
-        grouped_x = {}
-        latent_ps = {}
-        rope_ps = {}
-        kv_n = {}
-        flipped_n = {}
-        grouped_n = {}
-        grouped_b = {}
-        k_pe = {}
+        def regroup_a(g):
+            grouped = stage.tile(
+                [P, FUSED, PACK], BF16, align_bytes=64, tag="grouped_a", bufs=PASSES_A
+            )
+            for copy, cols in (
+                (nc.vector.tensor_copy, slice(0, A_SPLIT)),
+                (nc.scalar.copy, slice(A_SPLIT, FUSED)),
+            ):
+                copy(
+                    out=grouped[:, cols, :].rearrange("p (c i) t -> p c t i", i=RUN),
+                    in_=raw_a[g][:, :, cols].rearrange("p t (c i) -> p c t i", i=RUN),
+                )
+            grouped_a.append(grouped)
 
-        def flip_hidden(tt):
-            words = x_rows[tt][:].bitcast(F32)
-            grouped_x[tt] = stage.tile(
-                [P, PASSES_A * P * PACK], BF16, align_bytes=64, name="grouped_x", tag="grouped_x"
-            )
-            grouped_words = grouped_x[tt][:].bitcast(F32).rearrange(
-                "p (g k u) -> p g k u", g=PASSES_A, u=2
-            )
-            for b in range(2):
-                flipped = psum.tile([P, 2, 2, P], F32, tag="bank", bufs=4)
-                for gg in range(2):
-                    for u in range(2):
-                        first = (2 * b + gg) * (K_PASS // 2) + u * P
-                        nc.tensor.transpose(
-                            flipped[:, gg, u, :], words[:, first : first + P], ident_f32[:]
-                        )
-                nc.scalar.copy(
-                    out=grouped_words[:, 2 * b : 2 * b + 2, :, :],
-                    in_=flipped[:].rearrange("p g u k -> p g k u"),
+        def quantise_a(g):
+            for cols in (slice(0, LATENT), slice(LATENT, FUSED)):
+                nc.vector.quantize_mx(
+                    out=a_codes[:, g, cols].bitcast(FP8X4),
+                    scales=a_scales[:, g, cols],
+                    in_=grouped_a[g][:, cols, :].rearrange("p c t -> p (c t)"),
                 )
 
-        def quantise_hidden(tt):
-            nc.vector.quantize_mx(
-                out=x_codes[:, tt, :].bitcast(FP8X4), scales=x_scales[:, tt, :], in_=grouped_x[tt][:]
-            )
-
-        def first_product(tt):
-            latent_ps[tt] = psum.tile([P, LATENT], F32, name="latent_ps", tag="latent", bufs=2)
-            rope_ps[tt] = psum.tile([P, ROPE], F32, name="rope_ps", tag="rope", bufs=1)
-            for g in range(PASSES_A):
-                of_pass = slice(g * P, (g + 1) * P)
+        def first_product(g):
+            of_pass = slice(g * P, (g + 1) * P)
+            for tt in range(TOKEN_TILES):
+                if g == 0:
+                    latent_ps.append(psum.tile([P, LATENT], F32, name="latent_ps", tag="left"))
+                    rope_ps.append(psum.tile([P, ROPE], F32, name="rope_ps", tag="right"))
                 for acc, cols in (
                     (latent_ps[tt], slice(0, LATENT)),
                     (rope_ps[tt], slice(LATENT, FUSED)),
@@ -232,6 +211,24 @@ def tile_mla_pb_kernel(tc, hidden_states, w_kv_a, kv_a_ln_w, w_kv_b, out_0, out_
                         start=(g == 0),
                         stop=(g == PASSES_A - 1),
                     )
+
+        regroup_a(0)
+        for g in range(PASSES_A):
+            if g + 1 < PASSES_A:
+                regroup_a(g + 1)
+            quantise_a(g)
+            first_product(g)
+
+        n_codes = resident.tile([P, TOKEN_TILES, P], U32, align_bytes=64)
+        n_scales = resident.tile([P, TOKEN_TILES, P], U8, align_bytes=64)
+        b_codes = resident.tile([P, PIECES, KINDS, BANK], U32, align_bytes=64)
+        b_scales = resident.tile([P, PIECES, KINDS, BANK], U8, align_bytes=64)
+        kv_n = {}
+        flipped_n = {}
+        grouped_n = {}
+        grouped_b = {}
+        k_pe = {}
+        k_pieces = {}
 
         def root_mean_square(tt):
             squares = stage.tile([P, LATENT], BF16)
@@ -253,14 +250,14 @@ def tile_mla_pb_kernel(tc, hidden_states, w_kv_a, kv_a_ln_w, w_kv_b, out_0, out_
             )
 
         def flip_kv_n(tt):
-            flipped_n[tt] = psum.tile([P, PACK, P], BF16, name="flipped_n", tag="flipped_n", bufs=1)
+            flipped_n[tt] = psum.tile([P, PACK, P], BF16, name="flipped_n", tag="right")
             for t in range(PACK):
                 nc.tensor.transpose(
                     flipped_n[tt][:, t, :], kv_n[tt][:, t * P : (t + 1) * P], ident_bf16[:]
                 )
-
-        def regroup_kv_n(tt):
-            grouped_n[tt] = stage.tile([P, P, PACK], BF16, align_bytes=64, name="grouped_n", tag="grouped_n")
+            grouped_n[tt] = stage.tile(
+                [P, P, PACK], BF16, align_bytes=64, name="grouped_n", tag="grouped_n"
+            )
             nc.scalar.copy(out=grouped_n[tt][:], in_=flipped_n[tt][:].rearrange("p t k -> p k t"))
 
         def quantise_kv_n(tt):
@@ -283,88 +280,88 @@ def tile_mla_pb_kernel(tc, hidden_states, w_kv_a, kv_a_ln_w, w_kv_b, out_0, out_
             k_pe[tt] = consts.tile([P, 2, HALF], F32, name="k_pe%d" % tt)
             nc.gpsimd.tensor_tensor(out=k_pe[tt][:], in0=from_x1[:], in1=from_x2[:], op=ALU.add)
 
-        def bank_cols(j, b):
-            return slice(j * PIECE_COLS + b * BANK, j * PIECE_COLS + (b + 1) * BANK)
-
-        def regroup_b(j, b):
-            grouped_b[j, b] = stage.tile([P, BANK, PACK], BF16, align_bytes=64, name="grouped_b", tag="grouped_b")
-            regroup(nc.vector.tensor_copy, grouped_b[j, b][:], raw_b[j][:, :, b * BANK : (b + 1) * BANK])
-
-        def quantise_b(j, b):
-            nc.vector.quantize_mx(
-                out=b_codes[:, bank_cols(j, b)].bitcast(FP8X4),
-                scales=b_scales[:, bank_cols(j, b)],
-                in_=grouped_b[j, b][:].rearrange("p c t -> p (c t)"),
+        def spread_k_pe(j, tt):
+            k_pieces[j, tt] = pieces.tile(
+                [P, PIECE_HEADS, NOPE + ROPE], F32, name="k_piece", tag="k_piece"
             )
-
-        def prepare_b(j, turn):
-            if turn % 2 == 0:
-                regroup_b(j, turn // 2)
-            else:
-                quantise_b(j, turn // 2)
-
-        def second_product(j, tt):
-            if j + 1 < PIECES:
-                prepare_b(j + 1, tt)
-            k_piece = pieces.tile([P, PIECE_HEADS, NOPE + ROPE], F32)
-            v_piece = pieces.tile([P, PIECE_HEADS, V_DIM], F32)
             nc.gpsimd.tensor_scalar(
-                out=k_piece[:, :, NOPE:],
+                out=k_pieces[j, tt][:, :, NOPE:],
                 in0=k_pe[tt][:].rearrange("p h c -> p (h c)").unsqueeze(1).to_broadcast(
                     [P, PIECE_HEADS, ROPE]
                 ),
                 scalar1=1.0, scalar2=0.0, op0=ALU.mult, op1=ALU.add,
             )
-            for b in range(BANKS_PER_PIECE):
-                kv_ps = psum.tile([P, BANK], F32, tag="bank", bufs=4)
-                nc.tensor.matmul_mx(
-                    out=kv_ps[:],
-                    lhsT=n_codes[:, tt, :].bitcast(FP8X4),
-                    lhsT_scale=n_scales[:, tt, :],
-                    rhs=b_codes[:, bank_cols(j, b)].bitcast(FP8X4),
-                    rhs_scale=b_scales[:, bank_cols(j, b)],
-                    start=True,
-                    stop=True,
-                )
-                kv = kv_ps[:].rearrange("p (h s c) -> p h s c", h=BANK_HEADS, s=2)
-                in_piece = slice(b * BANK_HEADS, (b + 1) * BANK_HEADS)
-                to_vector = tt % 2 == 1 and b == BANKS_PER_PIECE - 1
-                copy = nc.vector.tensor_copy if to_vector else nc.scalar.copy
-                copy(out=k_piece[:, in_piece, :NOPE], in_=kv[:, :, 0, :])
-                copy(out=v_piece[:, in_piece, :], in_=kv[:, :, 1, :])
+
+        def regroup_b(j, kind):
+            grouped_b[j, kind] = stage.tile(
+                [P, BANK, PACK], BF16, align_bytes=64, name="grouped_b", tag="grouped_b"
+            )
+            by_kind = raw_b[j][:].rearrange(
+                "p t (h s c i) -> p s h c t i", h=PIECE_HEADS, s=KINDS, i=RUN
+            )
+            nc.vector.tensor_copy(
+                out=grouped_b[j, kind][:].rearrange("p (h c i) t -> p h c t i", h=PIECE_HEADS, i=RUN),
+                in_=by_kind[:, kind],
+            )
+
+        def quantise_b(j, kind):
+            nc.vector.quantize_mx(
+                out=b_codes[:, j, kind, :].bitcast(FP8X4),
+                scales=b_scales[:, j, kind, :],
+                in_=grouped_b[j, kind][:].rearrange("p c t -> p (c t)"),
+            )
+
+        def multiply_b(j, tt, kind, ring):
+            kv_ps = psum.tile([P, BANK], F32, name="kv_ps", tag=ring)
+            nc.tensor.matmul_mx(
+                out=kv_ps[:],
+                lhsT=n_codes[:, tt, :].bitcast(FP8X4),
+                lhsT_scale=n_scales[:, tt, :],
+                rhs=b_codes[:, j, kind, :].bitcast(FP8X4),
+                rhs_scale=b_scales[:, j, kind, :],
+                start=True,
+                stop=True,
+            )
+            return kv_ps[:].rearrange("p (h c) -> p h c", h=PIECE_HEADS)
+
+        def second_product(j, tt):
+            if j + 1 < PIECES:
+                if tt % 2 == 0:
+                    regroup_b(j + 1, tt // 2)
+                else:
+                    quantise_b(j + 1, tt // 2)
             tokens = slice(tt * P, (tt + 1) * P)
             heads = slice(j * PIECE_HEADS, (j + 1) * PIECE_HEADS)
-            nc.sync.dma_start(out=k_out[tokens, heads, :], in_=k_piece[:])
+            nc.scalar.copy(out=k_pieces[j, tt][:, :, :NOPE], in_=multiply_b(j, tt, KIND_K_NOPE, "left"))
+            nc.sync.dma_start(out=k_out[tokens, heads, :], in_=k_pieces[j, tt][:])
+            v_piece = pieces.tile([P, PIECE_HEADS, V_DIM], F32)
+            copy = nc.vector.tensor_copy if tt % 2 == 1 else nc.scalar.copy
+            copy(out=v_piece[:], in_=multiply_b(j, tt, KIND_V, "right"))
             nc.sync.dma_start(out=v_out[tokens, heads, :], in_=v_piece[:])
+
+        for kind in range(KINDS):
+            regroup_b(0, kind)
+        for kind in range(KINDS):
+            quantise_b(0, kind)
 
         def is_tile(tt):
             return 0 <= tt < TOKEN_TILES
 
-        flip_hidden(0)
-        flip_hidden(1)
-        quantise_hidden(0)
         for step in range(TOKEN_TILES + 4):
             if is_tile(step - 3):
                 quantise_kv_n(step - 3)
             if is_tile(step - 1):
                 normalise(step - 1)
-            if is_tile(step + 1):
-                quantise_hidden(step + 1)
-            if step < TOKEN_TILES:
-                prepare_b(0, step)
             if is_tile(step - 4):
                 second_product(0, step - 4)
             if is_tile(step):
-                first_product(step)
                 root_mean_square(step)
-            if is_tile(step + 2):
-                flip_hidden(step + 2)
+                rotate(step)
+                spread_k_pe(0, step)
             if is_tile(step - 2):
                 flip_kv_n(step - 2)
-                regroup_kv_n(step - 2)
-            if is_tile(step):
-                rotate(step)
 
         for j in range(1, PIECES):
             for tt in range(TOKEN_TILES):
+                spread_k_pe(j, tt)
                 second_product(j, tt)

@@ -168,7 +168,6 @@ def tile_mla_pb_kernel(tc, hidden_states, w_kv_a, kv_a_ln_w, w_kv_b, out_0, out_
         a_scales = resident.tile([P, PASSES_A, FUSED], U8, align_bytes=64)
         grouped_a = []
         latent_ps = []
-        rope_ps = []
 
         def regroup_a(g):
             grouped = stage.tile(
@@ -192,32 +191,31 @@ def tile_mla_pb_kernel(tc, hidden_states, w_kv_a, kv_a_ln_w, w_kv_b, out_0, out_
                     in_=grouped_a[g][:, cols, :].rearrange("p c t -> p (c t)"),
                 )
 
-        def first_product(g):
+        def first_product(acc, tt, g, cols):
             of_pass = slice(g * P, (g + 1) * P)
-            for tt in range(TOKEN_TILES):
-                if g == 0:
-                    latent_ps.append(psum.tile([P, LATENT], F32, name="latent_ps", tag="left"))
-                    rope_ps.append(psum.tile([P, ROPE], F32, name="rope_ps", tag="right"))
-                for acc, cols in (
-                    (latent_ps[tt], slice(0, LATENT)),
-                    (rope_ps[tt], slice(LATENT, FUSED)),
-                ):
-                    nc.tensor.matmul_mx(
-                        out=acc[:],
-                        lhsT=x_codes[:, tt, of_pass].bitcast(FP8X4),
-                        lhsT_scale=x_scales[:, tt, of_pass],
-                        rhs=a_codes[:, g, cols].bitcast(FP8X4),
-                        rhs_scale=a_scales[:, g, cols],
-                        start=(g == 0),
-                        stop=(g == PASSES_A - 1),
-                    )
+            nc.tensor.matmul_mx(
+                out=acc,
+                lhsT=x_codes[:, tt, of_pass].bitcast(FP8X4),
+                lhsT_scale=x_scales[:, tt, of_pass],
+                rhs=a_codes[:, g, cols].bitcast(FP8X4),
+                rhs_scale=a_scales[:, g, cols],
+                start=(g == 0),
+                stop=(g == PASSES_A - 1),
+            )
 
         regroup_a(0)
         for g in range(PASSES_A):
             if g + 1 < PASSES_A:
                 regroup_a(g + 1)
             quantise_a(g)
-            first_product(g)
+            for tt in range(TOKEN_TILES):
+                if g == 0:
+                    latent_ps.append(psum.tile([P, LATENT], F32, name="latent_ps", tag="left"))
+                first_product(latent_ps[tt][:], tt, g, slice(0, LATENT))
+        rope_ps = psum.tile([P, TOKEN_TILES, ROPE], F32, tag="right")
+        for tt in range(TOKEN_TILES):
+            for g in range(PASSES_A):
+                first_product(rope_ps[:, tt, :], tt, g, slice(LATENT, FUSED))
 
         n_codes = resident.tile([P, TOKEN_TILES, P], U32, align_bytes=64)
         n_scales = resident.tile([P, TOKEN_TILES, P], U8, align_bytes=64)
@@ -228,7 +226,7 @@ def tile_mla_pb_kernel(tc, hidden_states, w_kv_a, kv_a_ln_w, w_kv_b, out_0, out_
         grouped_n = {}
         grouped_b = {}
         k_pe = {}
-        k_pieces = {}
+        k_piece = {}
 
         def root_mean_square(tt):
             squares = stage.tile([P, LATENT], BF16)
@@ -269,7 +267,7 @@ def tile_mla_pb_kernel(tc, hidden_states, w_kv_a, kv_a_ln_w, w_kv_b, out_0, out_
 
         def rotate(tt):
             x = stage.tile([P, ROPE], F32, name="rope_x", tag="rope_x")
-            nc.scalar.copy(out=x[:], in_=rope_ps[tt][:])
+            nc.scalar.copy(out=x[:], in_=rope_ps[:, tt, :])
             a = tt % 2
             x1 = x[:, 0:HALF].unsqueeze(1).to_broadcast([P, 2, HALF])
             x2 = x[:, HALF:ROPE].unsqueeze(1).to_broadcast([P, 2, HALF])
@@ -280,12 +278,10 @@ def tile_mla_pb_kernel(tc, hidden_states, w_kv_a, kv_a_ln_w, w_kv_b, out_0, out_
             k_pe[tt] = consts.tile([P, 2, HALF], F32, name="k_pe%d" % tt)
             nc.gpsimd.tensor_tensor(out=k_pe[tt][:], in0=from_x1[:], in1=from_x2[:], op=ALU.add)
 
-        def spread_k_pe(j, tt):
-            k_pieces[j, tt] = pieces.tile(
-                [P, PIECE_HEADS, NOPE + ROPE], F32, name="k_piece", tag="k_piece"
-            )
+        def spread_k_pe(tt):
+            k_piece[tt] = resident.tile([P, PIECE_HEADS, NOPE + ROPE], F32, name="k_piece%d" % tt)
             nc.gpsimd.tensor_scalar(
-                out=k_pieces[j, tt][:, :, NOPE:],
+                out=k_piece[tt][:, :, NOPE:],
                 in0=k_pe[tt][:].rearrange("p h c -> p (h c)").unsqueeze(1).to_broadcast(
                     [P, PIECE_HEADS, ROPE]
                 ),
@@ -332,8 +328,8 @@ def tile_mla_pb_kernel(tc, hidden_states, w_kv_a, kv_a_ln_w, w_kv_b, out_0, out_
                     quantise_b(j + 1, tt // 2)
             tokens = slice(tt * P, (tt + 1) * P)
             heads = slice(j * PIECE_HEADS, (j + 1) * PIECE_HEADS)
-            nc.scalar.copy(out=k_pieces[j, tt][:, :, :NOPE], in_=multiply_b(j, tt, KIND_K_NOPE, "left"))
-            nc.sync.dma_start(out=k_out[tokens, heads, :], in_=k_pieces[j, tt][:])
+            nc.scalar.copy(out=k_piece[tt][:, :, :NOPE], in_=multiply_b(j, tt, KIND_K_NOPE, "left"))
+            nc.sync.dma_start(out=k_out[tokens, heads, :], in_=k_piece[tt][:])
             v_piece = pieces.tile([P, PIECE_HEADS, V_DIM], F32)
             copy = nc.vector.tensor_copy if tt % 2 == 1 else nc.scalar.copy
             copy(out=v_piece[:], in_=multiply_b(j, tt, KIND_V, "right"))
@@ -356,12 +352,12 @@ def tile_mla_pb_kernel(tc, hidden_states, w_kv_a, kv_a_ln_w, w_kv_b, out_0, out_
                 second_product(0, step - 4)
             if is_tile(step):
                 root_mean_square(step)
-                rotate(step)
-                spread_k_pe(0, step)
+            if is_tile(step - 1):
+                rotate(step - 1)
+                spread_k_pe(step - 1)
             if is_tile(step - 2):
                 flip_kv_n(step - 2)
 
         for j in range(1, PIECES):
             for tt in range(TOKEN_TILES):
-                spread_k_pe(j, tt)
                 second_product(j, tt)

@@ -60,7 +60,7 @@ def tile_mla_pb_kernel(tc, hidden_states, w_kv_a, kv_a_ln_w, w_kv_b, out_0, out_
         consts = ctx.enter_context(tc.tile_pool(name="consts", bufs=1))
         resident = ctx.enter_context(tc.tile_pool(name="resident", bufs=1))
         stage = ctx.enter_context(tc.tile_pool(name="stage", bufs=2))
-        pieces = ctx.enter_context(tc.tile_pool(name="pieces", bufs=6))
+        pieces = ctx.enter_context(tc.tile_pool(name="pieces", bufs=8))
         psum = ctx.enter_context(tc.psum_pool(name="psum", bufs=4))
 
         gain_row = consts.tile([P, LATENT], BF16)
@@ -139,12 +139,12 @@ def tile_mla_pb_kernel(tc, hidden_states, w_kv_a, kv_a_ln_w, w_kv_b, out_0, out_
 
         x_codes = resident.tile([P, TOKEN_TILES, PASSES_A * P], U32, align_bytes=64)
         x_scales = resident.tile([P, TOKEN_TILES, PASSES_A * P], U8, align_bytes=64)
-        for tt in range(TOKEN_TILES):
+        grouped_x = []
+
+        def flip_hidden(tt):
             words = x_rows[tt][:].bitcast(F32)
-            grouped_x = stage.tile([P, PASSES_A * P * PACK], BF16, align_bytes=64)
-            grouped_words = grouped_x[:].bitcast(F32).rearrange(
-                "p (g k u) -> p g k u", g=PASSES_A, u=2
-            )
+            grouped = stage.tile([P, PASSES_A * P * PACK], BF16, align_bytes=64, tag="grouped_x")
+            grouped_words = grouped[:].bitcast(F32).rearrange("p (g k u) -> p g k u", g=PASSES_A, u=2)
             for ring, copy, first_pass in (
                 ("left", nc.scalar.copy, 0),
                 ("right", nc.vector.tensor_copy, 2),
@@ -160,14 +160,21 @@ def tile_mla_pb_kernel(tc, hidden_states, w_kv_a, kv_a_ln_w, w_kv_b, out_0, out_
                     out=grouped_words[:, first_pass : first_pass + 2, :, :],
                     in_=flipped[:].rearrange("p g u k -> p g k u"),
                 )
+            grouped_x.append(grouped)
+
+        flip_hidden(0)
+        for tt in range(TOKEN_TILES):
+            if tt + 1 < TOKEN_TILES:
+                flip_hidden(tt + 1)
             nc.vector.quantize_mx(
-                out=x_codes[:, tt, :].bitcast(FP8X4), scales=x_scales[:, tt, :], in_=grouped_x[:]
+                out=x_codes[:, tt, :].bitcast(FP8X4), scales=x_scales[:, tt, :], in_=grouped_x[tt][:]
             )
 
         a_codes = resident.tile([P, PASSES_A, FUSED], U32, align_bytes=64)
         a_scales = resident.tile([P, PASSES_A, FUSED], U8, align_bytes=64)
         grouped_a = []
         latent_ps = []
+        rope_ps = []
 
         def regroup_a(g):
             grouped = stage.tile(
@@ -191,31 +198,32 @@ def tile_mla_pb_kernel(tc, hidden_states, w_kv_a, kv_a_ln_w, w_kv_b, out_0, out_
                     in_=grouped_a[g][:, cols, :].rearrange("p c t -> p (c t)"),
                 )
 
-        def first_product(acc, tt, g, cols):
+        def first_product(g):
             of_pass = slice(g * P, (g + 1) * P)
-            nc.tensor.matmul_mx(
-                out=acc,
-                lhsT=x_codes[:, tt, of_pass].bitcast(FP8X4),
-                lhsT_scale=x_scales[:, tt, of_pass],
-                rhs=a_codes[:, g, cols].bitcast(FP8X4),
-                rhs_scale=a_scales[:, g, cols],
-                start=(g == 0),
-                stop=(g == PASSES_A - 1),
-            )
+            for tt in range(TOKEN_TILES):
+                if g == 0:
+                    latent_ps.append(psum.tile([P, LATENT], F32, name="latent_ps", tag="left"))
+                    rope_ps.append(psum.tile([P, ROPE], F32, name="rope_ps", tag="right"))
+                for acc, cols in (
+                    (latent_ps[tt], slice(0, LATENT)),
+                    (rope_ps[tt], slice(LATENT, FUSED)),
+                ):
+                    nc.tensor.matmul_mx(
+                        out=acc[:],
+                        lhsT=x_codes[:, tt, of_pass].bitcast(FP8X4),
+                        lhsT_scale=x_scales[:, tt, of_pass],
+                        rhs=a_codes[:, g, cols].bitcast(FP8X4),
+                        rhs_scale=a_scales[:, g, cols],
+                        start=(g == 0),
+                        stop=(g == PASSES_A - 1),
+                    )
 
         regroup_a(0)
         for g in range(PASSES_A):
             if g + 1 < PASSES_A:
                 regroup_a(g + 1)
             quantise_a(g)
-            for tt in range(TOKEN_TILES):
-                if g == 0:
-                    latent_ps.append(psum.tile([P, LATENT], F32, name="latent_ps", tag="left"))
-                first_product(latent_ps[tt][:], tt, g, slice(0, LATENT))
-        rope_ps = psum.tile([P, TOKEN_TILES, ROPE], F32, tag="right")
-        for tt in range(TOKEN_TILES):
-            for g in range(PASSES_A):
-                first_product(rope_ps[:, tt, :], tt, g, slice(LATENT, FUSED))
+            first_product(g)
 
         n_codes = resident.tile([P, TOKEN_TILES, P], U32, align_bytes=64)
         n_scales = resident.tile([P, TOKEN_TILES, P], U8, align_bytes=64)
@@ -226,21 +234,25 @@ def tile_mla_pb_kernel(tc, hidden_states, w_kv_a, kv_a_ln_w, w_kv_b, out_0, out_
         grouped_n = {}
         grouped_b = {}
         k_pe = {}
-        k_piece = {}
+        k_pieces = {}
 
-        def root_mean_square(tt):
+        def sum_squares(tt):
             squares = stage.tile([P, LATENT], BF16)
             nc.scalar.activation(
                 out=squares[:], in_=latent_ps[tt][:], func=ACT.Square,
                 accum_out=square_sum[:, tt : tt + 1],
             )
+
+        def root_mean_square(tt):
             nc.scalar.activation(
                 out=rms[:, tt : tt + 1], in_=square_sum[:, tt : tt + 1], func=ACT.Sqrt,
                 bias=EPS, scale=1.0 / LATENT,
             )
 
-        def normalise(tt):
+        def invert_rms(tt):
             nc.vector.reciprocal(out=inv_rms[:, tt : tt + 1], in_=rms[:, tt : tt + 1])
+
+        def normalise(tt):
             kv_n[tt] = stage.tile([P, LATENT], BF16, name="kv_n", tag="kv_n")
             nc.vector.scalar_tensor_tensor(
                 out=kv_n[tt][:], in0=latent_ps[tt][:], scalar=inv_rms[:, tt : tt + 1], in1=gain[:],
@@ -267,7 +279,7 @@ def tile_mla_pb_kernel(tc, hidden_states, w_kv_a, kv_a_ln_w, w_kv_b, out_0, out_
 
         def rotate(tt):
             x = stage.tile([P, ROPE], F32, name="rope_x", tag="rope_x")
-            nc.scalar.copy(out=x[:], in_=rope_ps[:, tt, :])
+            nc.scalar.copy(out=x[:], in_=rope_ps[tt][:])
             a = tt % 2
             x1 = x[:, 0:HALF].unsqueeze(1).to_broadcast([P, 2, HALF])
             x2 = x[:, HALF:ROPE].unsqueeze(1).to_broadcast([P, 2, HALF])
@@ -278,10 +290,12 @@ def tile_mla_pb_kernel(tc, hidden_states, w_kv_a, kv_a_ln_w, w_kv_b, out_0, out_
             k_pe[tt] = consts.tile([P, 2, HALF], F32, name="k_pe%d" % tt)
             nc.gpsimd.tensor_tensor(out=k_pe[tt][:], in0=from_x1[:], in1=from_x2[:], op=ALU.add)
 
-        def spread_k_pe(tt):
-            k_piece[tt] = resident.tile([P, PIECE_HEADS, NOPE + ROPE], F32, name="k_piece%d" % tt)
+        def spread_k_pe(j, tt):
+            k_pieces[j, tt] = pieces.tile(
+                [P, PIECE_HEADS, NOPE + ROPE], F32, name="k_piece", tag="k_piece"
+            )
             nc.gpsimd.tensor_scalar(
-                out=k_piece[tt][:, :, NOPE:],
+                out=k_pieces[j, tt][:, :, NOPE:],
                 in0=k_pe[tt][:].rearrange("p h c -> p (h c)").unsqueeze(1).to_broadcast(
                     [P, PIECE_HEADS, ROPE]
                 ),
@@ -328,8 +342,8 @@ def tile_mla_pb_kernel(tc, hidden_states, w_kv_a, kv_a_ln_w, w_kv_b, out_0, out_
                     quantise_b(j + 1, tt // 2)
             tokens = slice(tt * P, (tt + 1) * P)
             heads = slice(j * PIECE_HEADS, (j + 1) * PIECE_HEADS)
-            nc.scalar.copy(out=k_piece[tt][:, :, :NOPE], in_=multiply_b(j, tt, KIND_K_NOPE, "left"))
-            nc.sync.dma_start(out=k_out[tokens, heads, :], in_=k_piece[tt][:])
+            nc.scalar.copy(out=k_pieces[j, tt][:, :, :NOPE], in_=multiply_b(j, tt, KIND_K_NOPE, "left"))
+            nc.sync.dma_start(out=k_out[tokens, heads, :], in_=k_pieces[j, tt][:])
             v_piece = pieces.tile([P, PIECE_HEADS, V_DIM], F32)
             copy = nc.vector.tensor_copy if tt % 2 == 1 else nc.scalar.copy
             copy(out=v_piece[:], in_=multiply_b(j, tt, KIND_V, "right"))
@@ -344,6 +358,8 @@ def tile_mla_pb_kernel(tc, hidden_states, w_kv_a, kv_a_ln_w, w_kv_b, out_0, out_
             return 0 <= tt < TOKEN_TILES
 
         for step in range(TOKEN_TILES + 4):
+            if is_tile(step - 1):
+                invert_rms(step - 1)
             if is_tile(step - 3):
                 quantise_kv_n(step - 3)
             if is_tile(step - 1):
@@ -351,13 +367,14 @@ def tile_mla_pb_kernel(tc, hidden_states, w_kv_a, kv_a_ln_w, w_kv_b, out_0, out_
             if is_tile(step - 4):
                 second_product(0, step - 4)
             if is_tile(step):
+                sum_squares(step)
+                rotate(step)
+                spread_k_pe(0, step)
                 root_mean_square(step)
-            if is_tile(step - 1):
-                rotate(step - 1)
-                spread_k_pe(step - 1)
             if is_tile(step - 2):
                 flip_kv_n(step - 2)
 
         for j in range(1, PIECES):
             for tt in range(TOKEN_TILES):
+                spread_k_pe(j, tt)
                 second_product(j, tt)

import math
from contextlib import ExitStack

import concourse.mybir as mybir
from concourse.masks import make_identity

F32 = mybir.dt.float32
BF16 = mybir.dt.bfloat16
I32 = mybir.dt.int32
U32 = mybir.dt.uint32
U8 = mybir.dt.uint8
FP8X4 = mybir.dt.float8_e4m3fn_x4
ALU = mybir.AluOpType
ACT = mybir.ActivationFunctionType

P = 128
PACK = 4
K_PASS = P * PACK
BANK = 512

TOKENS = 512
TOKEN_TILES = TOKENS // P
D_MODEL = 2048
PASSES_A = D_MODEL // K_PASS
LATENT = 512
ROPE = 128
HALF = ROPE // 2
HALF_LOG2 = 6
assert 2**HALF_LOG2 == HALF
FUSED = LATENT + ROPE
HEADS = 16
NOPE = 128
V_DIM = 128
KINDS = 2
KIND_K_NOPE = 0
KIND_V = 1
ROPE_BASE = 10000.0
EPS = 1e-6

PIECE_HEADS = BANK // NOPE
PIECE_COLS = PIECE_HEADS * (NOPE + V_DIM)
PIECES = HEADS // PIECE_HEADS

RUN = 4
A_SPLIT = FUSED // 2

ROUND_MAGIC = 1.5 * 2.0**23

FLOPS = 2 * TOKENS * D_MODEL * FUSED + 2 * TOKENS * LATENT * HEADS * (NOPE + V_DIM)


def tile_mla_pb_kernel(tc, hidden_states, w_kv_a, kv_a_ln_w, w_kv_b, out_0, out_1):
    nc = tc.nc
    hidden = hidden_states.flatten_outer_dims()
    k_out = out_0.rearrange("b s h c -> (b s) h c")
    v_out = out_1.rearrange("b s h c -> (b s) h c")

    with ExitStack() as ctx:
        ctx.enter_context(tc.manual_schedule())
        consts = ctx.enter_context(tc.tile_pool(name="consts", bufs=1))
        resident = ctx.enter_context(tc.tile_pool(name="resident", bufs=1))
        stage = ctx.enter_context(tc.tile_pool(name="stage", bufs=2))
        pieces = ctx.enter_context(tc.tile_pool(name="pieces", bufs=8))
        psum = ctx.enter_context(tc.psum_pool(name="psum", bufs=4))

        gain_row = consts.tile([P, LATENT], BF16)
        nc.vector.memset(gain_row[:], 0.0)
        x_rows = []
        for tt in range(TOKEN_TILES):
            rows = resident.tile([P, D_MODEL], BF16, name="x_rows%d" % tt)
            nc.sync.dma_start(out=rows[:], in_=hidden[tt * P : (tt + 1) * P, :])
            x_rows.append(rows)
            if tt == 0:
                nc.sync.dma_start(out=gain_row[0:1, :], in_=kv_a_ln_w.unsqueeze(0))
        raw_a = []
        for g in range(PASSES_A):
            raw = resident.tile([P, PACK, FUSED], BF16, name="raw_a%d" % g)
            rows = w_kv_a[g * K_PASS : (g + 1) * K_PASS, :]
            nc.sync.dma_start(
                out=raw[:].rearrange("p (u e) c -> p u e c", u=2),
                in_=rows.rearrange("(u q e) c -> q u e c", u=2, e=2),
            )
            raw_a.append(raw)
        raw_b = []
        for j in range(PIECES):
            raw = resident.tile([P, PACK, PIECE_COLS], BF16, name="raw_b%d" % j)
            cols = w_kv_b[:, j * PIECE_COLS : (j + 1) * PIECE_COLS]
            nc.sync.dma_start(out=raw[:], in_=cols.rearrange("(t p) n -> p t n", p=P))
            raw_b.append(raw)

        position = consts.tile([P, 2], I32)
        nc.gpsimd.iota(position[:], pattern=[[P, 2]], base=0, channel_multiplier=1)
        inv_freq = consts.tile([P, HALF], F32)
        nc.vector.memset(inv_freq[:, 0:1], 1.0)
        for level in range(HALF_LOG2):
            width = 2**level
            nc.vector.tensor_scalar(
                out=inv_freq[:, width : 2 * width], in0=inv_freq[:, 0:width],
                scalar1=ROPE_BASE ** (-width / HALF), scalar2=None, op0=ALU.mult,
            )
        position_turns = consts.tile([P, 2], F32)
        nc.vector.tensor_scalar(
            out=position_turns[:], in0=position[:], scalar1=1.0 / (2.0 * math.pi), scalar2=None,
            op0=ALU.mult,
        )
        phases = (0.5, 0.25, 0.0)
        turns = consts.tile([P, 2, len(phases), HALF], F32)
        for a in range(2):
            for i, phase in enumerate(phases):
                nc.vector.tensor_scalar(
                    out=turns[:, a, i, :], in0=inv_freq[:], scalar1=position_turns[:, a : a + 1],
                    scalar2=phase, op0=ALU.mult, op1=ALU.add,
                )
        whole_turns = consts.tile([P, 2, len(phases), HALF], F32)
        nc.vector.tensor_scalar(
            out=whole_turns[:], in0=turns[:], scalar1=ROUND_MAGIC, scalar2=ROUND_MAGIC,
            op0=ALU.add, op1=ALU.subtract,
        )
        part_turns = consts.tile([P, 2, len(phases), HALF], F32)
        nc.vector.tensor_tensor(out=part_turns[:], in0=turns[:], in1=whole_turns[:], op=ALU.subtract)
        table = consts.tile([P, 2, len(phases), HALF], F32)
        nc.scalar.activation(out=table[:], in_=part_turns[:], func=ACT.Sin, scale=2.0 * math.pi)

        square_sum = consts.tile([P, TOKEN_TILES], F32)
        rms = consts.tile([P, TOKEN_TILES], F32)
        inv_rms = consts.tile([P, TOKEN_TILES], F32)
        nc.scalar.activation(out=rms[:, 0:1], in_=inv_freq[:, 0:1], func=ACT.Sqrt)

        ident_f32 = consts.tile([P, P], F32)
        make_identity(nc, ident_f32[:])
        ident_bf16 = consts.tile([P, P], BF16)
        make_identity(nc, ident_bf16[:])
        ones = consts.tile([P, P], BF16)
        nc.vector.memset(ones[:], 1.0)
        gain_ps = psum.tile([P, LATENT], F32, tag="right")
        nc.tensor.matmul(out=gain_ps[:], lhsT=ones[:], rhs=gain_row[:], start=True, stop=True)
        gain = consts.tile([P, LATENT], BF16)
        nc.vector.tensor_copy(out=gain[:], in_=gain_ps[:])

        x_codes = resident.tile([P, TOKEN_TILES, PASSES_A * P], U32, align_bytes=64)
        x_scales = resident.tile([P, TOKEN_TILES, PASSES_A * P], U8, align_bytes=64)
        grouped_x = []

        def flip_hidden(tt):
            words = x_rows[tt][:].bitcast(F32)
            grouped = stage.tile([P, PASSES_A * P * PACK], BF16, align_bytes=64, tag="grouped_x")
            grouped_words = grouped[:].bitcast(F32).rearrange("p (g k u) -> p g k u", g=PASSES_A, u=2)
            for ring, copy, first_pass in (
                ("left", nc.scalar.copy, 0),
                ("right", nc.vector.tensor_copy, 2),
            ):
                flipped = psum.tile([P, 2, 2, P], F32, tag=ring)
                for gg in range(2):
                    for u in range(2):
                        first = (first_pass + gg) * (K_PASS // 2) + u * P
                        nc.tensor.transpose(
                            flipped[:, gg, u, :], words[:, first : first + P], ident_f32[:]
                        )
                copy(
                    out=grouped_words[:, first_pass : first_pass + 2, :, :],
                    in_=flipped[:].rearrange("p g u k -> p g k u"),
                )
            grouped_x.append(grouped)

        flip_hidden(0)
        for tt in range(TOKEN_TILES):
            if tt + 1 < TOKEN_TILES:
                flip_hidden(tt + 1)
            nc.vector.quantize_mx(
                out=x_codes[:, tt, :].bitcast(FP8X4), scales=x_scales[:, tt, :], in_=grouped_x[tt][:]
            )

        a_codes = resident.tile([P, PASSES_A, FUSED], U32, align_bytes=64)
        a_scales = resident.tile([P, PASSES_A, FUSED], U8, align_bytes=64)
        grouped_a = []
        latent_ps = []
        rope_ps = []

        def regroup_a(g):
            grouped = stage.tile(
                [P, FUSED, PACK], BF16, align_bytes=64, tag="grouped_a", bufs=PASSES_A
            )
            for copy, cols in (
                (nc.vector.tensor_copy, slice(0, A_SPLIT)),
                (nc.scalar.copy, slice(A_SPLIT, FUSED)),
            ):
                copy(
                    out=grouped[:, cols, :].rearrange("p (c i) t -> p c t i", i=RUN),
                    in_=raw_a[g][:, :, cols].rearrange("p t (c i) -> p c t i", i=RUN),
                )
            grouped_a.append(grouped)

        def quantise_a(g):
            for cols in (slice(0, LATENT), slice(LATENT, FUSED)):
                nc.vector.quantize_mx(
                    out=a_codes[:, g, cols].bitcast(FP8X4),
                    scales=a_scales[:, g, cols],
                    in_=grouped_a[g][:, cols, :].rearrange("p c t -> p (c t)"),
                )

        def first_product(g):
            of_pass = slice(g * P, (g + 1) * P)
            for tt in range(TOKEN_TILES):
                if g == 0:
                    latent_ps.append(psum.tile([P, LATENT], F32, name="latent_ps", tag="left"))
                    rope_ps.append(psum.tile([P, ROPE], F32, name="rope_ps", tag="right"))
                for acc, cols in (
                    (latent_ps[tt], slice(0, LATENT)),
                    (rope_ps[tt], slice(LATENT, FUSED)),
                ):
                    nc.tensor.matmul_mx(
                        out=acc[:],
                        lhsT=x_codes[:, tt, of_pass].bitcast(FP8X4),
                        lhsT_scale=x_scales[:, tt, of_pass],
                        rhs=a_codes[:, g, cols].bitcast(FP8X4),
                        rhs_scale=a_scales[:, g, cols],
                        start=(g == 0),
                        stop=(g == PASSES_A - 1),
                    )

        regroup_a(0)
        for g in range(PASSES_A):
            if g + 1 < PASSES_A:
                regroup_a(g + 1)
            quantise_a(g)
            first_product(g)

        n_codes = resident.tile([P, TOKEN_TILES, P], U32, align_bytes=64)
        n_scales = resident.tile([P, TOKEN_TILES, P], U8, align_bytes=64)
        b_codes = resident.tile([P, PIECES, KINDS, BANK], U32, align_bytes=64)
        b_scales = resident.tile([P, PIECES, KINDS, BANK], U8, align_bytes=64)
        kv_n = {}
        flipped_n = {}
        grouped_n = {}
        grouped_b = {}
        k_pe = {}
        k_pieces = {}

        def sum_squares(tt):
            squares = stage.tile([P, LATENT], BF16)
            nc.scalar.activation(
                out=squares[:], in_=latent_ps[tt][:], func=ACT.Square,
                accum_out=square_sum[:, tt : tt + 1],
            )

        def root_mean_square(tt):
            nc.scalar.activation(
                out=rms[:, tt : tt + 1], in_=square_sum[:, tt : tt + 1], func=ACT.Sqrt,
                bias=EPS, scale=1.0 / LATENT,
            )

        def invert_rms(tt):
            nc.vector.reciprocal(out=inv_rms[:, tt : tt + 1], in_=rms[:, tt : tt + 1])

        def normalise(tt):
            kv_n[tt] = stage.tile([P, LATENT], BF16, name="kv_n", tag="kv_n")
            nc.vector.scalar_tensor_tensor(
                out=kv_n[tt][:], in0=latent_ps[tt][:], scalar=inv_rms[:, tt : tt + 1], in1=gain[:],
                op0=ALU.mult, op1=ALU.mult,
            )

        def flip_kv_n(tt):
            flipped_n[tt] = psum.tile([P, PACK, P], BF16, name="flipped_n", tag="right")
            for t in range(PACK):
                nc.tensor.transpose(
                    flipped_n[tt][:, t, :], kv_n[tt][:, t * P : (t + 1) * P], ident_bf16[:]
                )
            grouped_n[tt] = stage.tile(
                [P, P, PACK], BF16, align_bytes=64, name="grouped_n", tag="grouped_n"
            )
            nc.scalar.copy(out=grouped_n[tt][:], in_=flipped_n[tt][:].rearrange("p t k -> p k t"))

        def quantise_kv_n(tt):
            nc.vector.quantize_mx(
                out=n_codes[:, tt, :].bitcast(FP8X4),
                scales=n_scales[:, tt, :],
                in_=grouped_n[tt][:].rearrange("p k t -> p (k t)"),
            )

        def rotate(tt):
            x = stage.tile([P, ROPE], F32, name="rope_x", tag="rope_x")
            nc.scalar.copy(out=x[:], in_=rope_ps[tt][:])
            a = tt % 2
            x1 = x[:, 0:HALF].unsqueeze(1).to_broadcast([P, 2, HALF])
            x2 = x[:, HALF:ROPE].unsqueeze(1).to_broadcast([P, 2, HALF])
            from_x1 = stage.tile([P, 2, HALF], F32)
            nc.gpsimd.tensor_tensor(out=from_x1[:], in0=x1, in1=table[:, a, 1:3, :], op=ALU.mult)
            from_x2 = stage.tile([P, 2, HALF], F32)
            nc.gpsimd.tensor_tensor(out=from_x2[:], in0=x2, in1=table[:, a, 0:2, :], op=ALU.mult)
            k_pe[tt] = consts.tile([P, 2, HALF], F32, name="k_pe%d" % tt)
            nc.gpsimd.tensor_tensor(out=k_pe[tt][:], in0=from_x1[:], in1=from_x2[:], op=ALU.add)

        def spread_k_pe(j, tt):
            k_pieces[j, tt] = pieces.tile(
                [P, PIECE_HEADS, NOPE + ROPE], F32, name="k_piece", tag="k_piece"
            )
            nc.gpsimd.tensor_scalar(
                out=k_pieces[j, tt][:, :, NOPE:],
                in0=k_pe[tt][:].rearrange("p h c -> p (h c)").unsqueeze(1).to_broadcast(
                    [P, PIECE_HEADS, ROPE]
                ),
                scalar1=1.0, scalar2=0.0, op0=ALU.mult, op1=ALU.add,
            )

        def regroup_b(j, kind):
            grouped_b[j, kind] = stage.tile(
                [P, BANK, PACK], BF16, align_bytes=64, name="grouped_b", tag="grouped_b"
            )
            by_kind = raw_b[j][:].rearrange(
                "p t (h s c i) -> p s h c t i", h=PIECE_HEADS, s=KINDS, i=RUN
            )
            nc.vector.tensor_copy(
                out=grouped_b[j, kind][:].rearrange("p (h c i) t -> p h c t i", h=PIECE_HEADS, i=RUN),
                in_=by_kind[:, kind],
            )

        def quantise_b(j, kind):
            nc.vector.quantize_mx(
                out=b_codes[:, j, kind, :].bitcast(FP8X4),
                scales=b_scales[:, j, kind, :],
                in_=grouped_b[j, kind][:].rearrange("p c t -> p (c t)"),
            )

        def multiply_b(j, tt, kind, ring):
            kv_ps = psum.tile([P, BANK], F32, name="kv_ps", tag=ring)
            nc.tensor.matmul_mx(
                out=kv_ps[:],
                lhsT=n_codes[:, tt, :].bitcast(FP8X4),
                lhsT_scale=n_scales[:, tt, :],
                rhs=b_codes[:, j, kind, :].bitcast(FP8X4),
                rhs_scale=b_scales[:, j, kind, :],
                start=True,
                stop=True,
            )
            return kv_ps[:].rearrange("p (h c) -> p h c", h=PIECE_HEADS)

        def second_product(j, tt):
            if j + 1 < PIECES:
                if tt % 2 == 0:
                    regroup_b(j + 1, tt // 2)
                else:
                    quantise_b(j + 1, tt // 2)
            tokens = slice(tt * P, (tt + 1) * P)
            heads = slice(j * PIECE_HEADS, (j + 1) * PIECE_HEADS)
            nc.scalar.copy(out=k_pieces[j, tt][:, :, :NOPE], in_=multiply_b(j, tt, KIND_K_NOPE, "left"))
            nc.sync.dma_start(out=k_out[tokens, heads, :], in_=k_pieces[j, tt][:])
            v_piece = pieces.tile([P, PIECE_HEADS, V_DIM], F32)
            copy = nc.vector.tensor_copy if tt % 2 == 1 else nc.scalar.copy
            copy(out=v_piece[:], in_=multiply_b(j, tt, KIND_V, "right"))
            nc.sync.dma_start(out=v_out[tokens, heads, :], in_=v_piece[:])

        for kind in range(KINDS):
            regroup_b(0, kind)
        for kind in range(KINDS):
            quantise_b(0, kind)

        def is_tile(tt):
            return 0 <= tt < TOKEN_TILES

        for step in range(TOKEN_TILES + 4):
            if is_tile(step - 1):
                invert_rms(step - 1)
            if is_tile(step - 3):
                quantise_kv_n(step - 3)
            if is_tile(step - 1):
                normalise(step - 1)
            if is_tile(step - 4):
                second_product(0, step - 4)
            if is_tile(step):
                sum_squares(step)
                rotate(step)
                spread_k_pe(0, step)
                root_mean_square(step)
            if is_tile(step - 2):
                flip_kv_n(step - 2)

        for j in range(1, PIECES):
            for tt in range(TOKEN_TILES):
                spread_k_pe(j, tt)
                second_product(j, tt)
